import numpy as np
import ml_dtypes


def mxq(x, axis, fmt="e4m3"):
    dtype, down = {"e4m3": (ml_dtypes.float8_e4m3fn, 7), "e5m2": (ml_dtypes.float8_e5m2, 14)}[fmt]
    v = np.moveaxis(np.asarray(x, np.float32).astype(ml_dtypes.bfloat16).astype(np.float64), axis, -1)
    blocks = v.reshape(v.shape[:-1] + (-1, 32))
    amax = np.abs(blocks).max(-1, keepdims=True)
    byte = np.maximum(np.where(amax > 0, np.frexp(amax)[1] - 1 + 127, 0) - down, 1)
    scale = np.exp2(byte - 127.0)
    codes = (blocks / scale).astype(np.float32).astype(dtype).astype(np.float64)
    return np.moveaxis((codes * scale).reshape(v.shape), -1, axis)


WIDE = False


def mx_kscale(k):
    if not WIDE:
        return np.ones(k)
    levels = np.array([10, -10, 5, -5, 0])
    if k % 512:
        return np.exp2(np.random.permutation(np.resize(levels, k // 32))).repeat(32)
    a = np.empty((k // 512, 16))
    for p in range(k // 512):
        a[p, :8] = np.random.permutation(np.resize(levels, 8))
        for g in range(8):
            far = levels[np.abs(levels - a[p, g]) >= 10]
            a[p, g + 8] = far[np.random.randint(len(far))]
    return np.exp2(a.ravel()).repeat(32)


BF16 = ml_dtypes.bfloat16


def bf(x):
    return np.asarray(x, np.float32).astype(BF16)


def f64(x):
    return np.asarray(x).astype(np.float64)


B, T, D, H, DH, F = 4, 1024, 512, 16, 64, 256
A = H * DH
EPS = 1e-6


def layer_norm(v, gain, bias):
    mu = v.mean(-1, keepdims=True)
    var = np.square(v - mu).mean(-1, keepdims=True)
    return (v - mu) * (1.0 / np.sqrt(var + EPS)) * gain + bias


def gelu_tanh(v):
    return 0.5 * v * (1.0 + np.tanh(np.sqrt(2.0 / np.pi) * (v + 0.044715 * v**3)))


def draw0():
    s, t = mx_kscale(A), mx_kscale(D)
    r = np.random.standard_normal
    return {"attn_out": bf(r((B, T, A)) * 0.3 * s),
            "residual": bf(r((B, T, D))),
            "wo": bf(r((A, D)) * 2.0 / np.sqrt(A) / s[:, None]),
            "bo": bf(0.1 * r(D)),
            "ln2_gain": bf((1.0 + 0.1 * r(D)) * t),
            "ln2_bias": bf(0.1 * r(D) * t),
            "w1": bf(r((D, F)) / np.sqrt(D) / t[:, None]),
            "b1": bf(0.1 * r(F))}


def core(attn_out, residual, wo, bo, ln2_gain, ln2_bias, w1, b1):
    x_mid = (mxq(f64(attn_out), 2, "e4m3") @ mxq(f64(wo), 0, "e4m3")) + f64(bo) + f64(residual)
    h = layer_norm(x_mid, f64(ln2_gain), f64(ln2_bias))
    g = gelu_tanh((mxq(h, 2, "e4m3") @ mxq(f64(w1), 0, "e4m3")) + f64(b1))
    return x_mid, g


def e4m3fn_bytes(y):
    return np.clip(np.asarray(y, np.float64), -448.0, 448.0).astype(np.float32).astype(ml_dtypes.float8_e4m3fn).view(np.uint8)


def e4m3fn_values(b):
    return np.asarray(b, np.uint8).view(ml_dtypes.float8_e4m3fn).astype(np.float64)


def setup_inputs():
    d = draw0()
    x0 = np.asarray(d['attn_out']).astype(np.float64)
    s = (np.max(np.abs(x0), axis=(0, 1), keepdims=True) / 448.0).astype(np.float32)
    out = {}
    for k, v in d.items():
        if k == 'attn_out':
            out['attn_out_bytes'] = e4m3fn_bytes(x0 / s.astype(np.float64))
            out['attn_out_scale'] = s
        else:
            out[k] = v
    return out


def reference(attn_out_bytes, attn_out_scale, residual, wo, bo, ln2_gain, ln2_bias, w1, b1):
    return core(e4m3fn_values(attn_out_bytes) * attn_out_scale.astype(np.float64), residual, wo, bo, ln2_gain, ln2_bias, w1, b1)

@@ -1,0 +1,400 @@
+from contextlib import ExitStack
+
+import concourse.mybir as mybir
+from concourse.masks import make_identity
+
+B, T, A, D, F = 4, 1024, 1024, 512, 256
+TOKENS = B * T
+EPS = 1e-6
+FLOPS = 2 * TOKENS * (A * D + D * F)
+
+F32 = mybir.dt.float32
+BF16 = mybir.dt.bfloat16
+U32 = mybir.dt.uint32
+U8 = mybir.dt.uint8
+FP8 = mybir.dt.float8_e4m3fn
+FP8X4 = mybir.dt.float8_e4m3fn_x4
+ALU = mybir.AluOpType
+ACT = mybir.ActivationFunctionType
+
+P = 128
+PACK = 4
+K_PASS = P * PACK
+A_PASSES = A // K_PASS
+TILES = TOKENS // P
+PAIRS = TILES // 2
+HALVES = F // P
+STAGE_SLOTS = 3
+
+
+def tile_swidtblock_pb_t_kernel(
+    tc, attn_out_bytes, attn_out_scale, residual, wo, bo, ln2_gain, ln2_bias, w1, b1, out_0, out_1
+):
+    nc = tc.nc
+    bytes_pairs = attn_out_bytes.rearrange("b (m r j) a -> (b m) r (j a)", r=P, j=2)
+    resid_pairs = residual.rearrange("b (m r j) d -> (b m) r (j d)", r=P, j=2)
+    x_rows = out_0.rearrange("b (m r j) d -> (b m) j r d", r=P, j=2)
+    g_pairs = out_1.rearrange("b (m r j) f -> (b m) r (j f)", r=P, j=2)
+
+    with ExitStack() as ctx:
+        keep = ctx.enter_context(tc.tile_pool(name="keep", bufs=1))
+        work = ctx.enter_context(tc.tile_pool(name="work", bufs=2))
+        psum = ctx.enter_context(tc.psum_pool(name="psum", bufs=1))
+        ctx.enter_context(tc.manual_schedule())
+
+        scale_col = keep.tile([P, A_PASSES, PACK], F32, name="scale_col")
+        nc.sync.dma_start(
+            out=scale_col[:], in_=attn_out_scale.rearrange("o q (g p t) -> p (o q g) t", p=P, t=PACK)
+        )
+        code_bytes = {}
+        resid = {}
+
+        def load_bytes(m):
+            code_bytes[m] = keep.tile([P, 2 * A], U8, name="code_bytes%d" % m)
+            nc.sync.dma_start(out=code_bytes[m][:], in_=bytes_pairs[m])
+
+        def load_resid(m):
+            resid[m] = keep.tile([P, 2 * D], BF16, name="resid%d" % m)
+            nc.sync.dma_start(out=resid[m][:], in_=resid_pairs[m])
+
+        def load_column(vec, width, name):
+            raw = keep.tile([P, width], BF16, name=name + "_raw")
+            nc.sync.dma_start(out=raw[:], in_=vec.rearrange("(p t) -> p t", t=width))
+            return raw
+
+        load_bytes(0)
+        wo_raw = []
+        for g in range(A_PASSES):
+            raw = keep.tile([P, PACK, D], BF16, name="wo_raw%d" % g)
+            nc.sync.dma_start(
+                out=raw[:], in_=wo[g * K_PASS : (g + 1) * K_PASS, :].rearrange("(p t) n -> p t n", t=PACK)
+            )
+            wo_raw.append(raw)
+        bo_raw = load_column(bo, PACK, "bo")
+        load_resid(0)
+        load_bytes(1)
+        load_resid(1)
+        gain_raw = load_column(ln2_gain, PACK, "gain")
+        bias_raw = load_column(ln2_bias, PACK, "bias")
+        b1_raw = load_column(b1, HALVES, "b1")
+        w1_raw = keep.tile([P, PACK, F], BF16, name="w1_raw")
+        nc.sync.dma_start(out=w1_raw[:], in_=w1.rearrange("(p t) f -> p t f", t=PACK))
+        for m in range(2, PAIRS):
+            load_bytes(m)
+            load_resid(m)
+
+        ident = keep.tile([P, P], F32, name="ident")
+        make_identity(nc, ident[:])
+        minus_half = keep.tile([P, 2], F32, name="minus_half")
+        nc.gpsimd.memset(minus_half[:], -0.5)
+
+        def widen_column(raw, width, name):
+            col = keep.tile([P, width], F32, name=name + "_col")
+            nc.gpsimd.tensor_copy(out=col[:], in_=raw[:])
+            return col
+
+        scale_banks = []
+        for g in range(A_PASSES):
+            bank = psum.tile([P, P, PACK], F32, name="scale_bank%d" % g)
+            for t in range(PACK):
+                nc.tensor.transpose(
+                    bank[:, :, t], scale_col[:, g, t : t + 1].to_broadcast([P, P]), ident[:]
+                )
+            scale_banks.append(bank)
+
+        bo_col = widen_column(bo_raw, PACK, "bo")
+        gain_col = widen_column(gain_raw, PACK, "gain")
+        bias_col = widen_column(bias_raw, PACK, "bias")
+        b1_col = widen_column(b1_raw, HALVES, "b1")
+        bo_rows = keep.tile([P, D], F32, name="bo_rows")
+
+        def spread_bo():
+            bank = psum.tile([P, PACK, P], F32, name="bo_bank", tag="g_bank")
+            for t in range(PACK):
+                nc.tensor.transpose(bank[:, t, :], bo_col[:, t : t + 1].to_broadcast([P, P]), ident[:])
+            nc.scalar.copy(
+                out=bo_rows[:].rearrange("r (m t) -> r m t", t=PACK), in_=bank[:].rearrange("r t m -> r m t")
+            )
+
+        wo_codes = [keep.tile([P, D], U32, name="wo_codes%d" % g, align_bytes=64) for g in range(A_PASSES)]
+        wo_scales = [keep.tile([P, D], U8, name="wo_scales%d" % g, align_bytes=64) for g in range(A_PASSES)]
+        w1_codes = keep.tile([P, F], U32, name="w1_codes", align_bytes=64)
+        w1_scales = keep.tile([P, F], U8, name="w1_scales", align_bytes=64)
+        wo_grouped = {}
+        HALF_D = D // 2
+
+        def interleave_wo(g, half):
+            grouped = keep.tile([P, HALF_D, PACK], BF16, name="wo_grouped%d_%d" % (g, half), align_bytes=64)
+            dst = grouped[:].rearrange("p (c i) t -> p c t i", i=4)
+            src = wo_raw[g][:, :, half * HALF_D : (half + 1) * HALF_D].rearrange("p t (c i) -> p c t i", i=4)
+            if half == 0:
+                nc.scalar.copy(out=dst, in_=src)
+            else:
+                nc.vector.tensor_copy(out=dst, in_=src)
+            wo_grouped[(g, half)] = grouped
+
+        def quantize_wo(g, half):
+            cols = slice(half * HALF_D, (half + 1) * HALF_D)
+            nc.vector.quantize_mx(
+                out=wo_codes[g][:, cols].bitcast(FP8X4),
+                scales=wo_scales[g][:, cols],
+                in_=wo_grouped[(g, half)][:].rearrange("p n t -> p (n t)"),
+            )
+
+        w1_grouped = keep.tile([P, HALVES, P, PACK], BF16, name="w1_grouped", align_bytes=64)
+
+        def interleave_w1():
+            nc.scalar.copy(out=w1_grouped[:], in_=w1_raw[:].rearrange("p t (m h) -> p h m t", h=HALVES))
+
+        def quantize_w1():
+            nc.vector.quantize_mx(
+                out=w1_codes[:].bitcast(FP8X4),
+                scales=w1_scales[:],
+                in_=w1_grouped[:].rearrange("p h m t -> p (h m t)"),
+            )
+
+        a_rows, a_bank, a_grouped, a_codes, a_scales = {}, {}, {}, {}, {}
+        base, mm_bank, x, n_rows = {}, {}, {}, {}
+        sums, squares, variance, rstd, shift = {}, {}, {}, {}, {}
+        n_banks, h_planes, h_grouped, h_codes, h_scales = {}, {}, {}, {}, {}
+        up_bank, g_cols, g_bank = {}, {}, {}
+
+        def scale_attn(i):
+            m, j = divmod(i, 2)
+            a_rows[i] = work.tile([P, A], BF16, name="a_rows")
+            for g in range(A_PASSES):
+                start = j * A + g * K_PASS
+                codes = code_bytes[m][:, start : start + K_PASS].bitcast(FP8)
+                nc.vector.tensor_tensor(
+                    out=a_rows[i][:, g * K_PASS : (g + 1) * K_PASS],
+                    in0=codes,
+                    in1=scale_banks[g][:].rearrange("r p t -> r (p t)"),
+                    op=ALU.mult,
+                )
+
+        def transpose_attn(i):
+            words = a_rows[i][:].bitcast(F32)
+            a_bank[i] = psum.tile([P, A_PASSES, 2, P], F32, name="a_bank")
+            for g in range(A_PASSES):
+                for u in range(2):
+                    nc.tensor.transpose(
+                        a_bank[i][:, g, u, :], words[:, 2 * P * g + u : 2 * P * (g + 1) : 2], ident[:]
+                    )
+
+        def group_attn(i):
+            a_grouped[i] = keep.tile([P, A], BF16, name="a_grouped", tag="stage%d" % (i % STAGE_SLOTS), align_bytes=64)
+            nc.scalar.copy(
+                out=a_grouped[i][:].bitcast(F32).rearrange("p (g r u) -> p g r u", g=A_PASSES, u=2),
+                in_=a_bank[i][:].rearrange("p g u r -> p g r u"),
+            )
+
+        def quantize_attn(i):
+            a_codes[i] = work.tile([P, A_PASSES * P], U32, name="a_codes", align_bytes=64)
+            a_scales[i] = work.tile([P, A_PASSES * P], U8, name="a_scales", align_bytes=64)
+            nc.vector.quantize_mx(out=a_codes[i][:].bitcast(FP8X4), scales=a_scales[i][:], in_=a_grouped[i][:])
+
+        def add_bo(i):
+            m, j = divmod(i, 2)
+            base[i] = keep.tile([P, D], F32, name="base", tag="stage%d" % (i % STAGE_SLOTS), align_bytes=64)
+            nc.gpsimd.tensor_tensor(out=base[i][:], in0=resid[m][:, j * D : (j + 1) * D], in1=bo_rows[:], op=ALU.add)
+
+        def project(i):
+            mm_bank[i] = psum.tile([P, D], F32, name="mm_bank")
+            for g in range(A_PASSES):
+                cols = slice(g * P, (g + 1) * P)
+                nc.tensor.matmul_mx(
+                    out=mm_bank[i][:],
+                    lhsT=a_codes[i][:, cols].bitcast(FP8X4),
+                    lhsT_scale=a_scales[i][:, cols],
+                    rhs=wo_codes[g][:].bitcast(FP8X4),
+                    rhs_scale=wo_scales[g][:],
+                    start=(g == 0),
+                    stop=(g == A_PASSES - 1),
+                )
+
+        def finish_x(i):
+            m, j = divmod(i, 2)
+            if j == 0:
+                sums[m] = work.tile([P, 2], F32, name="sums", bufs=3)
+            x[i] = work.tile([P, D], F32, name="x", bufs=10)
+            nc.vector.scalar_tensor_tensor(
+                out=x[i][:],
+                in0=mm_bank[i][:],
+                scalar=1.0,
+                in1=base[i][:],
+                op0=ALU.mult,
+                op1=ALU.add,
+                accum_out=sums[m][:, j : j + 1],
+            )
+            nc.sync.dma_start(out=x_rows[m, j], in_=x[i][:])
+
+        def square_sums(i):
+            m, j = divmod(i, 2)
+            if j == 0:
+                squares[m] = work.tile([P, 2], F32, name="squares")
+            deviations = work.tile([P, D], BF16, name="deviations")
+            nc.scalar.activation(
+                out=deviations[:],
+                in_=x[i][:],
+                func=ACT.Square,
+                scale=-float(D),
+                bias=sums[m][:, j : j + 1],
+                accum_out=squares[m][:, j : j + 1],
+            )
+
+        def variance_of(m):
+            variance[m] = work.tile([P, 2], F32, name="variance")
+            nc.scalar.activation(
+                out=variance[m][:], in_=squares[m][:], func=ACT.Identity, scale=1.0 / D**3, bias=EPS
+            )
+
+        def inverse_root(m):
+            rstd[m] = work.tile([P, 2], F32, name="rstd")
+            nc.gpsimd.tensor_tensor(out=rstd[m][:], in0=variance[m][:], in1=minus_half[:], op=ALU.pow)
+
+        def shift_of(m):
+            shift[m] = work.tile([P, 2], F32, name="shift")
+            nc.vector.scalar_tensor_tensor(
+                out=shift[m][:], in0=sums[m][:], scalar=-1.0 / D, in1=rstd[m][:], op0=ALU.mult, op1=ALU.mult
+            )
+
+        def normalise(i):
+            m, j = divmod(i, 2)
+            n_rows[i] = work.tile([P, PACK, P], F32, name="n_rows%d" % j)
+            dst = n_rows[i][:].rearrange("r t (c e) -> r c t e", e=2)
+            src = x[i][:].rearrange("r (c e t) -> r c t e", e=2, t=PACK)
+            if j == 0:
+                nc.scalar.activation(
+                    out=dst, in_=src, func=ACT.Identity, scale=rstd[m][:, j : j + 1], bias=shift[m][:, j : j + 1]
+                )
+            else:
+                nc.vector.tensor_scalar(
+                    out=dst,
+                    in0=src,
+                    scalar1=rstd[m][:, j : j + 1],
+                    scalar2=shift[m][:, j : j + 1],
+                    op0=ALU.mult,
+                    op1=ALU.add,
+                )
+
+        def transpose_n(m):
+            n_banks[m] = [psum.tile([P, 2, 2 * P], F32, name="n_bank%d" % q) for q in range(2)]
+            for t in range(PACK):
+                for j in range(2):
+                    nc.tensor.transpose(
+                        n_banks[m][t // 2][:, t % 2, j * P : (j + 1) * P], n_rows[2 * m + j][:, t, :], ident[:]
+                    )
+
+        def gain_and_bias(m):
+            h_planes[m] = work.tile([P, PACK, 2 * P], BF16, name="h_planes")
+            for t in range(PACK):
+                nc.scalar.activation(
+                    out=h_planes[m][:, t, :],
+                    in_=n_banks[m][t // 2][:, t % 2, :],
+                    func=ACT.Identity,
+                    scale=gain_col[:, t : t + 1],
+                    bias=bias_col[:, t : t + 1],
+                )
+
+        def group_h(m):
+            h_grouped[m] = work.tile([P, 2 * P, PACK], BF16, name="h_grouped", align_bytes=64)
+            nc.vector.tensor_copy(
+                out=h_grouped[m][:].rearrange("p (c i) t -> p c t i", i=4),
+                in_=h_planes[m][:].rearrange("p t (c i) -> p c t i", i=4),
+            )
+
+        def quantize_h(m):
+            h_codes[m] = work.tile([P, 2 * P], U32, name="h_codes", align_bytes=64)
+            h_scales[m] = work.tile([P, 2 * P], U8, name="h_scales", align_bytes=64)
+            nc.vector.quantize_mx(
+                out=h_codes[m][:].bitcast(FP8X4),
+                scales=h_scales[m][:],
+                in_=h_grouped[m][:].rearrange("p c t -> p (c t)"),
+            )
+
+        def up_project(m):
+            up_bank[m] = psum.tile([P, HALVES, 2 * P], F32, name="up_bank")
+            for h in range(HALVES):
+                cols = slice(h * P, (h + 1) * P)
+                nc.tensor.matmul_mx(
+                    out=up_bank[m][:, h, :],
+                    lhsT=w1_codes[:, cols].bitcast(FP8X4),
+                    lhsT_scale=w1_scales[:, cols],
+                    rhs=h_codes[m][:].bitcast(FP8X4),
+                    rhs_scale=h_scales[m][:],
+                    start=True,
+                    stop=True,
+                )
+
+        def gelu(m):
+            g_cols[m] = work.tile([P, HALVES, 2 * P], F32, name="g_cols")
+            for h in range(HALVES):
+                nc.scalar.activation(
+                    out=g_cols[m][:, h, :],
+                    in_=up_bank[m][:, h, :],
+                    func=ACT.Gelu_apprx_tanh,
+                    bias=b1_col[:, h : h + 1],
+                )
+
+        def transpose_g(m):
+            g_bank[m] = psum.tile([P, 2, HALVES, P], F32, name="g_bank", tag="g_bank")
+            for j in range(2):
+                for h in range(HALVES):
+                    nc.tensor.transpose(g_bank[m][:, j, h, :], g_cols[m][:, h, j * P : (j + 1) * P], ident[:])
+
+        def store_g(m):
+            g_rows = work.tile([P, 2, P, HALVES], F32, name="g_rows", bufs=3)
+            nc.scalar.copy(out=g_rows[:], in_=g_bank[m][:].rearrange("r j h m -> r j m h"))
+            nc.sync.dma_start(out=g_pairs[m], in_=g_rows[:].rearrange("r j m h -> r (j m h)"))
+
+        def for_tile(stage, i):
+            if 0 <= i < TILES:
+                stage(i)
+
+        def for_pair(stage, step, lag):
+            m, odd = divmod(step - lag - 1, 2)
+            if odd == 0 and 0 <= m < PAIRS:
+                stage(m)
+
+        def normalise_first(m):
+            normalise(2 * m)
+
+        def normalise_second(m):
+            normalise(2 * m + 1)
+
+        for s in range(TILES + 10):
+            for_tile(finish_x, s - 3)
+            if s == 1:
+                spread_bo()
+            for_tile(add_bo, s - 2)
+            for_pair(variance_of, s, 4)
+            for_tile(group_attn, s - 1)
+            for_pair(inverse_root, s, 4)
+            for_tile(project, s - 2)
+            for_pair(up_project, s, 9)
+            if s < A_PASSES:
+                interleave_wo(s, 0)
+            for_tile(scale_attn, s)
+            if s < A_PASSES:
+                interleave_wo(s, 1)
+            if s == 1:
+                for g in range(A_PASSES):
+                    for half in range(2):
+                        quantize_wo(g, half)
+            if s == 2:
+                interleave_w1()
+            if s == 4:
+                quantize_w1()
+            for_pair(gain_and_bias, s, 6)
+            for_pair(normalise_first, s, 5)
+            for_tile(square_sums, s - 3)
+            for_pair(transpose_g, s, 10)
+            for_tile(transpose_attn, s)
+            for_pair(store_g, s, 10)
+            for_pair(gelu, s, 9)
+            for_pair(quantize_h, s, 8)
+            for_pair(shift_of, s, 4)
+            for_pair(group_h, s, 7)
+            for_pair(normalise_second, s, 5)
+            for_tile(quantize_attn, s - 1)
+            for_pair(transpose_n, s, 5)

@@ -25,6 +25,7 @@ TILES = TOKENS // P
 PAIRS = TILES // 2
 HALVES = F // P
 STAGE_SLOTS = 3
+GROUP_ON_SCALAR = 64
 
 
 def tile_swidtblock_pb_t_kernel(
@@ -62,14 +63,17 @@ def tile_swidtblock_pb_t_kernel(
             nc.sync.dma_start(out=raw[:], in_=vec.rearrange("(p t) -> p t", t=width))
             return raw
 
-        load_bytes(0)
-        wo_raw = []
-        for g in range(A_PASSES):
-            raw = keep.tile([P, PACK, D], BF16, name="wo_raw%d" % g)
+        wo_raw = {}
+
+        def load_wo(g):
+            wo_raw[g] = keep.tile([P, PACK, D], BF16, name="wo_raw%d" % g)
             nc.sync.dma_start(
-                out=raw[:], in_=wo[g * K_PASS : (g + 1) * K_PASS, :].rearrange("(p t) n -> p t n", t=PACK)
+                out=wo_raw[g][:], in_=wo[g * K_PASS : (g + 1) * K_PASS, :].rearrange("(p t) n -> p t n", t=PACK)
             )
-            wo_raw.append(raw)
+
+        load_wo(0)
+        load_bytes(0)
+        load_wo(1)
         bo_raw = load_column(bo, PACK, "bo")
         load_resid(0)
         load_bytes(1)
@@ -107,13 +111,14 @@ def tile_swidtblock_pb_t_kernel(
         bias_col = widen_column(bias_raw, PACK, "bias")
         b1_col = widen_column(b1_raw, HALVES, "b1")
         bo_rows = keep.tile([P, D], F32, name="bo_rows")
+        b1_rows = keep.tile([P, F], F32, name="b1_rows")
 
-        def spread_bo():
-            bank = psum.tile([P, PACK, P], F32, name="bo_bank", tag="g_bank")
-            for t in range(PACK):
-                nc.tensor.transpose(bank[:, t, :], bo_col[:, t : t + 1].to_broadcast([P, P]), ident[:])
+        def spread(col, width, rows):
+            bank = psum.tile([P, width, P], F32, name="spread_bank", tag="up_bank")
+            for t in range(width):
+                nc.tensor.transpose(bank[:, t, :], col[:, t : t + 1].to_broadcast([P, P]), ident[:])
             nc.scalar.copy(
-                out=bo_rows[:].rearrange("r (m t) -> r m t", t=PACK), in_=bank[:].rearrange("r t m -> r m t")
+                out=rows[:].rearrange("r (m t) -> r m t", t=width), in_=bank[:].rearrange("r t m -> r m t")
             )
 
         wo_codes = [keep.tile([P, D], U32, name="wo_codes%d" % g, align_bytes=64) for g in range(A_PASSES)]
@@ -141,23 +146,26 @@ def tile_swidtblock_pb_t_kernel(
                 in_=wo_grouped[(g, half)][:].rearrange("p n t -> p (n t)"),
             )
 
-        w1_grouped = keep.tile([P, HALVES, P, PACK], BF16, name="w1_grouped", align_bytes=64)
+        w1_grouped = keep.tile([P, F, PACK], BF16, name="w1_grouped", align_bytes=64)
 
         def interleave_w1():
-            nc.scalar.copy(out=w1_grouped[:], in_=w1_raw[:].rearrange("p t (m h) -> p h m t", h=HALVES))
+            nc.scalar.copy(
+                out=w1_grouped[:].rearrange("p (c i) t -> p c t i", i=4),
+                in_=w1_raw[:].rearrange("p t (c i) -> p c t i", i=4),
+            )
 
         def quantize_w1():
             nc.vector.quantize_mx(
                 out=w1_codes[:].bitcast(FP8X4),
                 scales=w1_scales[:],
-                in_=w1_grouped[:].rearrange("p h m t -> p (h m t)"),
+                in_=w1_grouped[:].rearrange("p f t -> p (f t)"),
             )
 
         a_rows, a_bank, a_grouped, a_codes, a_scales = {}, {}, {}, {}, {}
         base, mm_bank, x, n_rows = {}, {}, {}, {}
         sums, squares, variance, rstd, shift = {}, {}, {}, {}, {}
         n_banks, h_planes, h_grouped, h_codes, h_scales = {}, {}, {}, {}, {}
-        up_bank, g_cols, g_bank = {}, {}, {}
+        up_bank, pre_gelu = {}, {}
 
         def scale_attn(i):
             m, j = divmod(i, 2)
@@ -199,7 +207,7 @@ def tile_swidtblock_pb_t_kernel(
             nc.gpsimd.tensor_tensor(out=base[i][:], in0=resid[m][:, j * D : (j + 1) * D], in1=bo_rows[:], op=ALU.add)
 
         def project(i):
-            mm_bank[i] = psum.tile([P, D], F32, name="mm_bank")
+            mm_bank[i] = psum.tile([P, D], F32, name="mm_bank", bufs=2)
             for g in range(A_PASSES):
                 cols = slice(g * P, (g + 1) * P)
                 nc.tensor.matmul_mx(
@@ -258,12 +266,12 @@ def tile_swidtblock_pb_t_kernel(
                 out=shift[m][:], in0=sums[m][:], scalar=-1.0 / D, in1=rstd[m][:], op0=ALU.mult, op1=ALU.mult
             )
 
-        def normalise(i):
+        def normalise(i, on_scalar):
             m, j = divmod(i, 2)
             n_rows[i] = work.tile([P, PACK, P], F32, name="n_rows%d" % j)
             dst = n_rows[i][:].rearrange("r t (c e) -> r c t e", e=2)
             src = x[i][:].rearrange("r (c e t) -> r c t e", e=2, t=PACK)
-            if j == 0:
+            if on_scalar:
                 nc.scalar.activation(
                     out=dst, in_=src, func=ACT.Identity, scale=rstd[m][:, j : j + 1], bias=shift[m][:, j : j + 1]
                 )
@@ -298,10 +306,14 @@ def tile_swidtblock_pb_t_kernel(
 
         def group_h(m):
             h_grouped[m] = work.tile([P, 2 * P, PACK], BF16, name="h_grouped", align_bytes=64)
-            nc.vector.tensor_copy(
-                out=h_grouped[m][:].rearrange("p (c i) t -> p c t i", i=4),
-                in_=h_planes[m][:].rearrange("p t (c i) -> p c t i", i=4),
-            )
+            for copy, cols in (
+                (nc.scalar.copy, slice(0, GROUP_ON_SCALAR)),
+                (nc.vector.tensor_copy, slice(GROUP_ON_SCALAR, 2 * P)),
+            ):
+                copy(
+                    out=h_grouped[m][:, cols, :].rearrange("p (c i) t -> p c t i", i=4),
+                    in_=h_planes[m][:, :, cols].rearrange("p t (c i) -> p c t i", i=4),
+                )
 
         def quantize_h(m):
             h_codes[m] = work.tile([P, 2 * P], U32, name="h_codes", align_bytes=64)
@@ -313,39 +325,34 @@ def tile_swidtblock_pb_t_kernel(
             )
 
         def up_project(m):
-            up_bank[m] = psum.tile([P, HALVES, 2 * P], F32, name="up_bank")
-            for h in range(HALVES):
-                cols = slice(h * P, (h + 1) * P)
+            up_bank[m] = psum.tile([P, 2, F], F32, name="up_bank", tag="up_bank")
+            for j in range(2):
+                cols = slice(j * P, (j + 1) * P)
                 nc.tensor.matmul_mx(
-                    out=up_bank[m][:, h, :],
-                    lhsT=w1_codes[:, cols].bitcast(FP8X4),
-                    lhsT_scale=w1_scales[:, cols],
-                    rhs=h_codes[m][:].bitcast(FP8X4),
-                    rhs_scale=h_scales[m][:],
+                    out=up_bank[m][:, j, :],
+                    lhsT=h_codes[m][:, cols].bitcast(FP8X4),
+                    lhsT_scale=h_scales[m][:, cols],
+                    rhs=w1_codes[:].bitcast(FP8X4),
+                    rhs_scale=w1_scales[:],
                     start=True,
                     stop=True,
                 )
 
+        def add_b1(m):
+            pre_gelu[m] = work.tile([P, 2, F], F32, name="pre_gelu")
+            nc.vector.tensor_tensor(
+                out=pre_gelu[m][:],
+                in0=up_bank[m][:],
+                in1=b1_rows[:].unsqueeze(1).to_broadcast([P, 2, F]),
+                op=ALU.add,
+            )
+
         def gelu(m):
-            g_cols[m] = work.tile([P, HALVES, 2 * P], F32, name="g_cols")
-            for h in range(HALVES):
-                nc.scalar.activation(
-                    out=g_cols[m][:, h, :],
-                    in_=up_bank[m][:, h, :],
-                    func=ACT.Gelu_apprx_tanh,
-                    bias=b1_col[:, h : h + 1],
-                )
-
-        def transpose_g(m):
-            g_bank[m] = psum.tile([P, 2, HALVES, P], F32, name="g_bank", tag="g_bank")
-            for j in range(2):
-                for h in range(HALVES):
-                    nc.tensor.transpose(g_bank[m][:, j, h, :], g_cols[m][:, h, j * P : (j + 1) * P], ident[:])
-
-        def store_g(m):
-            g_rows = work.tile([P, 2, P, HALVES], F32, name="g_rows", bufs=3)
-            nc.scalar.copy(out=g_rows[:], in_=g_bank[m][:].rearrange("r j h m -> r j m h"))
-            nc.sync.dma_start(out=g_pairs[m], in_=g_rows[:].rearrange("r j m h -> r (j m h)"))
+            g_rows = work.tile([P, 2 * F], F32, name="g_rows", bufs=3)
+            nc.scalar.activation(
+                out=g_rows[:], in_=pre_gelu[m][:].rearrange("r j f -> r (j f)"), func=ACT.Gelu_apprx_tanh
+            )
+            nc.sync.dma_start(out=g_pairs[m], in_=g_rows[:])
 
         def for_tile(stage, i):
             if 0 <= i < TILES:
@@ -356,45 +363,50 @@ def tile_swidtblock_pb_t_kernel(
             if odd == 0 and 0 <= m < PAIRS:
                 stage(m)
 
-        def normalise_first(m):
-            normalise(2 * m)
+        def normalise_pair_on_scalar(m):
+            normalise(2 * m, True)
+            normalise(2 * m + 1, True)
 
-        def normalise_second(m):
-            normalise(2 * m + 1)
+        def normalise_pair_shared(m):
+            normalise(2 * m, True)
+            normalise(2 * m + 1, False)
 
-        for s in range(TILES + 10):
+        for s in range(TILES + 11):
             for_tile(finish_x, s - 3)
             if s == 1:
-                spread_bo()
+                spread(bo_col, PACK, bo_rows)
+            if s == 3:
+                spread(b1_col, HALVES, b1_rows)
             for_tile(add_bo, s - 2)
             for_pair(variance_of, s, 4)
             for_tile(group_attn, s - 1)
             for_pair(inverse_root, s, 4)
             for_tile(project, s - 2)
             for_pair(up_project, s, 9)
-            if s < A_PASSES:
-                interleave_wo(s, 0)
+            if s == 0:
+                interleave_wo(0, 0)
+                interleave_wo(1, 0)
+                interleave_wo(0, 1)
             for_tile(scale_attn, s)
-            if s < A_PASSES:
-                interleave_wo(s, 1)
+            if s == 0:
+                interleave_wo(1, 1)
+                quantize_wo(0, 0)
+                quantize_wo(0, 1)
             if s == 1:
-                for g in range(A_PASSES):
-                    for half in range(2):
-                        quantize_wo(g, half)
+                quantize_wo(1, 1)
+                quantize_wo(1, 0)
             if s == 2:
                 interleave_w1()
             if s == 4:
                 quantize_w1()
+            for_pair(add_b1, s, 10)
             for_pair(gain_and_bias, s, 6)
-            for_pair(normalise_first, s, 5)
+            for_pair(normalise_pair_on_scalar if s < TILES else normalise_pair_shared, s, 5)
             for_tile(square_sums, s - 3)
-            for_pair(transpose_g, s, 10)
             for_tile(transpose_attn, s)
-            for_pair(store_g, s, 10)
-            for_pair(gelu, s, 9)
+            for_pair(gelu, s, 11)
             for_pair(quantize_h, s, 8)
             for_pair(shift_of, s, 4)
             for_pair(group_h, s, 7)
-            for_pair(normalise_second, s, 5)
             for_tile(quantize_attn, s - 1)
             for_pair(transpose_n, s, 5)

@@ -25,7 +25,7 @@ TILES = TOKENS // P
 PAIRS = TILES // 2
 HALVES = F // P
 STAGE_SLOTS = 3
-GROUP_ON_SCALAR = 64
+GPSIMD_BASE_TILES = 2
 
 
 def tile_swidtblock_pb_t_kernel(
@@ -89,6 +89,8 @@ def tile_swidtblock_pb_t_kernel(
 
         ident = keep.tile([P, P], F32, name="ident")
         make_identity(nc, ident[:])
+        ident_bf16 = keep.tile([P, P], BF16, name="ident_bf16")
+        make_identity(nc, ident_bf16[:])
         minus_half = keep.tile([P, 2], F32, name="minus_half")
         nc.gpsimd.memset(minus_half[:], -0.5)
 
@@ -120,6 +122,14 @@ def tile_swidtblock_pb_t_kernel(
             nc.scalar.copy(
                 out=rows[:].rearrange("r (m t) -> r m t", t=width), in_=bank[:].rearrange("r t m -> r m t")
             )
+
+        bo_blocks = keep.tile([P, D // P, P], F32, name="bo_blocks")
+
+        def turn_bo():
+            bank = psum.tile([P, D // P, P], F32, name="bo_bank", tag="up_bank")
+            for c in range(D // P):
+                nc.tensor.transpose(bank[:, c, :], bo_rows[:, c * P : (c + 1) * P], ident[:])
+            nc.scalar.copy(out=bo_blocks[:], in_=bank[:])
 
         wo_codes = [keep.tile([P, D], U32, name="wo_codes%d" % g, align_bytes=64) for g in range(A_PASSES)]
         wo_scales = [keep.tile([P, D], U8, name="wo_scales%d" % g, align_bytes=64) for g in range(A_PASSES)]
@@ -162,10 +172,13 @@ def tile_swidtblock_pb_t_kernel(
             )
 
         a_rows, a_bank, a_grouped, a_codes, a_scales = {}, {}, {}, {}, {}
-        base, mm_bank, x, n_rows = {}, {}, {}, {}
+        base, base_bank, mm_bank, x, n_rows = {}, {}, {}, {}, {}
         sums, squares, variance, rstd, shift = {}, {}, {}, {}, {}
         n_banks, h_planes, h_grouped, h_codes, h_scales = {}, {}, {}, {}, {}
         up_bank, pre_gelu = {}, {}
+
+        def stage_tile(shape, dtype, name, i):
+            return keep.tile(shape, dtype, name=name, tag="stage%d" % (i % STAGE_SLOTS), align_bytes=64)
 
         def scale_attn(i):
             m, j = divmod(i, 2)
@@ -190,7 +203,7 @@ def tile_swidtblock_pb_t_kernel(
                     )
 
         def group_attn(i):
-            a_grouped[i] = keep.tile([P, A], BF16, name="a_grouped", tag="stage%d" % (i % STAGE_SLOTS), align_bytes=64)
+            a_grouped[i] = stage_tile([P, A], BF16, "a_grouped", i)
             nc.scalar.copy(
                 out=a_grouped[i][:].bitcast(F32).rearrange("p (g r u) -> p g r u", g=A_PASSES, u=2),
                 in_=a_bank[i][:].rearrange("p g u r -> p g r u"),
@@ -201,13 +214,33 @@ def tile_swidtblock_pb_t_kernel(
             a_scales[i] = work.tile([P, A_PASSES * P], U8, name="a_scales", align_bytes=64)
             nc.vector.quantize_mx(out=a_codes[i][:].bitcast(FP8X4), scales=a_scales[i][:], in_=a_grouped[i][:])
 
-        def add_bo(i):
+        def base_on_gpsimd(i):
             m, j = divmod(i, 2)
-            base[i] = keep.tile([P, D], F32, name="base", tag="stage%d" % (i % STAGE_SLOTS), align_bytes=64)
+            base[i] = stage_tile([P, D], F32, "first_base", i)
             nc.gpsimd.tensor_tensor(out=base[i][:], in0=resid[m][:, j * D : (j + 1) * D], in1=bo_rows[:], op=ALU.add)
 
+        def base_on_tensor(i):
+            m, j = divmod(i, 2)
+            base_bank[i] = psum.tile([P, D], F32, name="base_bank")
+            nc.tensor.matmul(
+                out=base_bank[i][:], lhsT=ident_bf16[:], rhs=resid[m][:, j * D : (j + 1) * D], start=True, stop=False
+            )
+            for c in range(D // P):
+                nc.tensor.matmul(
+                    out=base_bank[i][:, c * P : (c + 1) * P],
+                    lhsT=bo_blocks[:, c, :],
+                    rhs=ident[:],
+                    is_transpose=True,
+                    start=False,
+                    stop=(c == D // P - 1),
+                )
+
+        def fetch_base(i):
+            base[i] = work.tile([P, D], F32, name="base", bufs=3)
+            nc.scalar.copy(out=base[i][:], in_=base_bank[i][:])
+
         def project(i):
-            mm_bank[i] = psum.tile([P, D], F32, name="mm_bank", bufs=2)
+            mm_bank[i] = psum.tile([P, D], F32, name="mm_bank")
             for g in range(A_PASSES):
                 cols = slice(g * P, (g + 1) * P)
                 nc.tensor.matmul_mx(
@@ -266,24 +299,24 @@ def tile_swidtblock_pb_t_kernel(
                 out=shift[m][:], in0=sums[m][:], scalar=-1.0 / D, in1=rstd[m][:], op0=ALU.mult, op1=ALU.mult
             )
 
-        def normalise(i, on_scalar):
+        def normalise(i, engine, rows):
             m, j = divmod(i, 2)
-            n_rows[i] = work.tile([P, PACK, P], F32, name="n_rows%d" % j)
-            dst = n_rows[i][:].rearrange("r t (c e) -> r c t e", e=2)
+            n_rows[i] = rows
+            dst = rows[:].rearrange("r t (c e) -> r c t e", e=2)
             src = x[i][:].rearrange("r (c e t) -> r c t e", e=2, t=PACK)
-            if on_scalar:
-                nc.scalar.activation(
-                    out=dst, in_=src, func=ACT.Identity, scale=rstd[m][:, j : j + 1], bias=shift[m][:, j : j + 1]
-                )
+            scale, bias = rstd[m][:, j : j + 1], shift[m][:, j : j + 1]
+            if engine is nc.scalar:
+                engine.activation(out=dst, in_=src, func=ACT.Identity, scale=scale, bias=bias)
             else:
-                nc.vector.tensor_scalar(
-                    out=dst,
-                    in0=src,
-                    scalar1=rstd[m][:, j : j + 1],
-                    scalar2=shift[m][:, j : j + 1],
-                    op0=ALU.mult,
-                    op1=ALU.add,
-                )
+                engine.tensor_scalar(out=dst, in0=src, scalar1=scale, scalar2=bias, op0=ALU.mult, op1=ALU.add)
+
+        def normalise_on_gpsimd(m):
+            normalise(2 * m, nc.gpsimd, stage_tile([P, PACK, P], F32, "n_rows_staged", 2 * m + 4))
+            normalise(2 * m + 1, nc.gpsimd, work.tile([P, PACK, P], F32, name="n_rows1"))
+
+        def normalise_shared(m):
+            normalise(2 * m, nc.scalar, work.tile([P, PACK, P], F32, name="n_rows0"))
+            normalise(2 * m + 1, nc.vector, work.tile([P, PACK, P], F32, name="n_rows1"))
 
         def transpose_n(m):
             n_banks[m] = [psum.tile([P, 2, 2 * P], F32, name="n_bank%d" % q) for q in range(2)]
@@ -304,16 +337,23 @@ def tile_swidtblock_pb_t_kernel(
                     bias=bias_col[:, t : t + 1],
                 )
 
-        def group_h(m):
+        def group_h_on_gpsimd(m):
+            h_grouped[m] = stage_tile([P, 2 * P, PACK], BF16, "h_grouped_staged", 2 * m + 7)
+            nc.gpsimd.tensor_scalar(
+                out=h_grouped[m][:],
+                in0=h_planes[m][:].rearrange("p t c -> p c t"),
+                scalar1=1.0,
+                scalar2=0.0,
+                op0=ALU.mult,
+                op1=ALU.add,
+            )
+
+        def group_h_on_vector(m):
             h_grouped[m] = work.tile([P, 2 * P, PACK], BF16, name="h_grouped", align_bytes=64)
-            for copy, cols in (
-                (nc.scalar.copy, slice(0, GROUP_ON_SCALAR)),
-                (nc.vector.tensor_copy, slice(GROUP_ON_SCALAR, 2 * P)),
-            ):
-                copy(
-                    out=h_grouped[m][:, cols, :].rearrange("p (c i) t -> p c t i", i=4),
-                    in_=h_planes[m][:, :, cols].rearrange("p t (c i) -> p c t i", i=4),
-                )
+            nc.vector.tensor_copy(
+                out=h_grouped[m][:].rearrange("p (c i) t -> p c t i", i=4),
+                in_=h_planes[m][:].rearrange("p t (c i) -> p c t i", i=4),
+            )
 
         def quantize_h(m):
             h_codes[m] = work.tile([P, 2 * P], U32, name="h_codes", align_bytes=64)
@@ -363,26 +403,28 @@ def tile_swidtblock_pb_t_kernel(
             if odd == 0 and 0 <= m < PAIRS:
                 stage(m)
 
-        def normalise_pair_on_scalar(m):
-            normalise(2 * m, True)
-            normalise(2 * m + 1, True)
-
-        def normalise_pair_shared(m):
-            normalise(2 * m, True)
-            normalise(2 * m + 1, False)
-
         for s in range(TILES + 11):
             for_tile(finish_x, s - 3)
             if s == 1:
                 spread(bo_col, PACK, bo_rows)
             if s == 3:
                 spread(b1_col, HALVES, b1_rows)
-            for_tile(add_bo, s - 2)
+            if s == 2:
+                turn_bo()
+            if s - 2 < GPSIMD_BASE_TILES:
+                for_tile(base_on_gpsimd, s - 2)
+            else:
+                for_tile(fetch_base, s - 2)
+            if s <= TILES:
+                for_pair(normalise_on_gpsimd, s, 5)
+                for_pair(group_h_on_gpsimd, s, 8)
             for_pair(variance_of, s, 4)
             for_tile(group_attn, s - 1)
             for_pair(inverse_root, s, 4)
             for_tile(project, s - 2)
             for_pair(up_project, s, 9)
+            if s - 1 >= GPSIMD_BASE_TILES:
+                for_tile(base_on_tensor, s - 1)
             if s == 0:
                 interleave_wo(0, 0)
                 interleave_wo(1, 0)
@@ -401,12 +443,14 @@ def tile_swidtblock_pb_t_kernel(
                 quantize_w1()
             for_pair(add_b1, s, 10)
             for_pair(gain_and_bias, s, 6)
-            for_pair(normalise_pair_on_scalar if s < TILES else normalise_pair_shared, s, 5)
+            if s > TILES:
+                for_pair(normalise_shared, s, 5)
             for_tile(square_sums, s - 3)
             for_tile(transpose_attn, s)
             for_pair(gelu, s, 11)
             for_pair(quantize_h, s, 8)
             for_pair(shift_of, s, 4)
-            for_pair(group_h, s, 7)
+            if s >= TILES:
+                for_pair(group_h_on_vector, s, 7)
             for_tile(quantize_attn, s - 1)
             for_pair(transpose_n, s, 5)

from contextlib import ExitStack

import concourse.mybir as mybir
from concourse.masks import make_identity

B, T, A, D, F = 4, 1024, 1024, 512, 256
TOKENS = B * T
EPS = 1e-6
FLOPS = 2 * TOKENS * (A * D + D * F)

F32 = mybir.dt.float32
BF16 = mybir.dt.bfloat16
U32 = mybir.dt.uint32
U8 = mybir.dt.uint8
FP8 = mybir.dt.float8_e4m3fn
FP8X4 = mybir.dt.float8_e4m3fn_x4
ALU = mybir.AluOpType
ACT = mybir.ActivationFunctionType

P = 128
PACK = 4
K_PASS = P * PACK
A_PASSES = A // K_PASS
TILES = TOKENS // P
PAIRS = TILES // 2
HALVES = F // P
STAGE_SLOTS = 3
GPSIMD_BASE_TILES = 2


def tile_swidtblock_pb_t_kernel(
    tc, attn_out_bytes, attn_out_scale, residual, wo, bo, ln2_gain, ln2_bias, w1, b1, out_0, out_1
):
    nc = tc.nc
    bytes_pairs = attn_out_bytes.rearrange("b (m r j) a -> (b m) r (j a)", r=P, j=2)
    resid_pairs = residual.rearrange("b (m r j) d -> (b m) r (j d)", r=P, j=2)
    x_rows = out_0.rearrange("b (m r j) d -> (b m) j r d", r=P, j=2)
    g_pairs = out_1.rearrange("b (m r j) f -> (b m) r (j f)", r=P, j=2)

    with ExitStack() as ctx:
        keep = ctx.enter_context(tc.tile_pool(name="keep", bufs=1))
        work = ctx.enter_context(tc.tile_pool(name="work", bufs=2))
        psum = ctx.enter_context(tc.psum_pool(name="psum", bufs=1))
        ctx.enter_context(tc.manual_schedule())

        scale_col = keep.tile([P, A_PASSES, PACK], F32, name="scale_col")
        nc.sync.dma_start(
            out=scale_col[:], in_=attn_out_scale.rearrange("o q (g p t) -> p (o q g) t", p=P, t=PACK)
        )
        code_bytes = {}
        resid = {}

        def load_bytes(m):
            code_bytes[m] = keep.tile([P, 2 * A], U8, name="code_bytes%d" % m)
            nc.sync.dma_start(out=code_bytes[m][:], in_=bytes_pairs[m])

        def load_resid(m):
            resid[m] = keep.tile([P, 2 * D], BF16, name="resid%d" % m)
            nc.sync.dma_start(out=resid[m][:], in_=resid_pairs[m])

        def load_column(vec, width, name):
            raw = keep.tile([P, width], BF16, name=name + "_raw")
            nc.sync.dma_start(out=raw[:], in_=vec.rearrange("(p t) -> p t", t=width))
            return raw

        wo_raw = {}

        def load_wo(g):
            wo_raw[g] = keep.tile([P, PACK, D], BF16, name="wo_raw%d" % g)
            nc.sync.dma_start(
                out=wo_raw[g][:], in_=wo[g * K_PASS : (g + 1) * K_PASS, :].rearrange("(p t) n -> p t n", t=PACK)
            )

        load_wo(0)
        load_bytes(0)
        load_wo(1)
        bo_raw = load_column(bo, PACK, "bo")
        load_resid(0)
        load_bytes(1)
        load_resid(1)
        gain_raw = load_column(ln2_gain, PACK, "gain")
        bias_raw = load_column(ln2_bias, PACK, "bias")
        b1_raw = load_column(b1, HALVES, "b1")
        w1_raw = keep.tile([P, PACK, F], BF16, name="w1_raw")
        nc.sync.dma_start(out=w1_raw[:], in_=w1.rearrange("(p t) f -> p t f", t=PACK))
        for m in range(2, PAIRS):
            load_bytes(m)
            load_resid(m)

        ident = keep.tile([P, P], F32, name="ident")
        make_identity(nc, ident[:])
        ident_bf16 = keep.tile([P, P], BF16, name="ident_bf16")
        make_identity(nc, ident_bf16[:])
        minus_half = keep.tile([P, 2], F32, name="minus_half")
        nc.gpsimd.memset(minus_half[:], -0.5)

        def widen_column(raw, width, name):
            col = keep.tile([P, width], F32, name=name + "_col")
            nc.gpsimd.tensor_copy(out=col[:], in_=raw[:])
            return col

        scale_banks = []
        for g in range(A_PASSES):
            bank = psum.tile([P, P, PACK], F32, name="scale_bank%d" % g)
            for t in range(PACK):
                nc.tensor.transpose(
                    bank[:, :, t], scale_col[:, g, t : t + 1].to_broadcast([P, P]), ident[:]
                )
            scale_banks.append(bank)

        bo_col = widen_column(bo_raw, PACK, "bo")
        gain_col = widen_column(gain_raw, PACK, "gain")
        bias_col = widen_column(bias_raw, PACK, "bias")
        b1_col = widen_column(b1_raw, HALVES, "b1")
        bo_rows = keep.tile([P, D], F32, name="bo_rows")
        b1_rows = keep.tile([P, F], F32, name="b1_rows")

        def spread(col, width, rows):
            bank = psum.tile([P, width, P], F32, name="spread_bank", tag="up_bank")
            for t in range(width):
                nc.tensor.transpose(bank[:, t, :], col[:, t : t + 1].to_broadcast([P, P]), ident[:])
            nc.scalar.copy(
                out=rows[:].rearrange("r (m t) -> r m t", t=width), in_=bank[:].rearrange("r t m -> r m t")
            )

        bo_blocks = keep.tile([P, D // P, P], F32, name="bo_blocks")

        def turn_bo():
            bank = psum.tile([P, D // P, P], F32, name="bo_bank", tag="up_bank")
            for c in range(D // P):
                nc.tensor.transpose(bank[:, c, :], bo_rows[:, c * P : (c + 1) * P], ident[:])
            nc.scalar.copy(out=bo_blocks[:], in_=bank[:])

        wo_codes = [keep.tile([P, D], U32, name="wo_codes%d" % g, align_bytes=64) for g in range(A_PASSES)]
        wo_scales = [keep.tile([P, D], U8, name="wo_scales%d" % g, align_bytes=64) for g in range(A_PASSES)]
        w1_codes = keep.tile([P, F], U32, name="w1_codes", align_bytes=64)
        w1_scales = keep.tile([P, F], U8, name="w1_scales", align_bytes=64)
        wo_grouped = {}
        HALF_D = D // 2

        def interleave_wo(g, half):
            grouped = keep.tile([P, HALF_D, PACK], BF16, name="wo_grouped%d_%d" % (g, half), align_bytes=64)
            dst = grouped[:].rearrange("p (c i) t -> p c t i", i=4)
            src = wo_raw[g][:, :, half * HALF_D : (half + 1) * HALF_D].rearrange("p t (c i) -> p c t i", i=4)
            if half == 0:
                nc.scalar.copy(out=dst, in_=src)
            else:
                nc.vector.tensor_copy(out=dst, in_=src)
            wo_grouped[(g, half)] = grouped

        def quantize_wo(g, half):
            cols = slice(half * HALF_D, (half + 1) * HALF_D)
            nc.vector.quantize_mx(
                out=wo_codes[g][:, cols].bitcast(FP8X4),
                scales=wo_scales[g][:, cols],
                in_=wo_grouped[(g, half)][:].rearrange("p n t -> p (n t)"),
            )

        w1_grouped = keep.tile([P, F, PACK], BF16, name="w1_grouped", align_bytes=64)

        def interleave_w1():
            nc.scalar.copy(
                out=w1_grouped[:].rearrange("p (c i) t -> p c t i", i=4),
                in_=w1_raw[:].rearrange("p t (c i) -> p c t i", i=4),
            )

        def quantize_w1():
            nc.vector.quantize_mx(
                out=w1_codes[:].bitcast(FP8X4),
                scales=w1_scales[:],
                in_=w1_grouped[:].rearrange("p f t -> p (f t)"),
            )

        a_rows, a_bank, a_grouped, a_codes, a_scales = {}, {}, {}, {}, {}
        base, base_bank, mm_bank, x, n_rows = {}, {}, {}, {}, {}
        sums, squares, variance, rstd, shift = {}, {}, {}, {}, {}
        n_banks, h_planes, h_grouped, h_codes, h_scales = {}, {}, {}, {}, {}
        up_bank, pre_gelu = {}, {}

        def stage_tile(shape, dtype, name, i):
            return keep.tile(shape, dtype, name=name, tag="stage%d" % (i % STAGE_SLOTS), align_bytes=64)

        def scale_attn(i):
            m, j = divmod(i, 2)
            a_rows[i] = work.tile([P, A], BF16, name="a_rows")
            for g in range(A_PASSES):
                start = j * A + g * K_PASS
                codes = code_bytes[m][:, start : start + K_PASS].bitcast(FP8)
                nc.vector.tensor_tensor(
                    out=a_rows[i][:, g * K_PASS : (g + 1) * K_PASS],
                    in0=codes,
                    in1=scale_banks[g][:].rearrange("r p t -> r (p t)"),
                    op=ALU.mult,
                )

        def transpose_attn(i):
            words = a_rows[i][:].bitcast(F32)
            a_bank[i] = psum.tile([P, A_PASSES, 2, P], F32, name="a_bank")
            for g in range(A_PASSES):
                for u in range(2):
                    nc.tensor.transpose(
                        a_bank[i][:, g, u, :], words[:, 2 * P * g + u : 2 * P * (g + 1) : 2], ident[:]
                    )

        def group_attn(i):
            a_grouped[i] = stage_tile([P, A], BF16, "a_grouped", i)
            nc.scalar.copy(
                out=a_grouped[i][:].bitcast(F32).rearrange("p (g r u) -> p g r u", g=A_PASSES, u=2),
                in_=a_bank[i][:].rearrange("p g u r -> p g r u"),
            )

        def quantize_attn(i):
            a_codes[i] = work.tile([P, A_PASSES * P], U32, name="a_codes", align_bytes=64)
            a_scales[i] = work.tile([P, A_PASSES * P], U8, name="a_scales", align_bytes=64)
            nc.vector.quantize_mx(out=a_codes[i][:].bitcast(FP8X4), scales=a_scales[i][:], in_=a_grouped[i][:])

        def base_on_gpsimd(i):
            m, j = divmod(i, 2)
            base[i] = stage_tile([P, D], F32, "first_base", i)
            nc.gpsimd.tensor_tensor(out=base[i][:], in0=resid[m][:, j * D : (j + 1) * D], in1=bo_rows[:], op=ALU.add)

        def base_on_tensor(i):
            m, j = divmod(i, 2)
            base_bank[i] = psum.tile([P, D], F32, name="base_bank")
            nc.tensor.matmul(
                out=base_bank[i][:], lhsT=ident_bf16[:], rhs=resid[m][:, j * D : (j + 1) * D], start=True, stop=False
            )
            for c in range(D // P):
                nc.tensor.matmul(
                    out=base_bank[i][:, c * P : (c + 1) * P],
                    lhsT=bo_blocks[:, c, :],
                    rhs=ident[:],
                    is_transpose=True,
                    start=False,
                    stop=(c == D // P - 1),
                )

        def fetch_base(i):
            base[i] = work.tile([P, D], F32, name="base", bufs=3)
            nc.scalar.copy(out=base[i][:], in_=base_bank[i][:])

        def project(i):
            mm_bank[i] = psum.tile([P, D], F32, name="mm_bank")
            for g in range(A_PASSES):
                cols = slice(g * P, (g + 1) * P)
                nc.tensor.matmul_mx(
                    out=mm_bank[i][:],
                    lhsT=a_codes[i][:, cols].bitcast(FP8X4),
                    lhsT_scale=a_scales[i][:, cols],
                    rhs=wo_codes[g][:].bitcast(FP8X4),
                    rhs_scale=wo_scales[g][:],
                    start=(g == 0),
                    stop=(g == A_PASSES - 1),
                )

        def finish_x(i):
            m, j = divmod(i, 2)
            if j == 0:
                sums[m] = work.tile([P, 2], F32, name="sums", bufs=3)
            x[i] = work.tile([P, D], F32, name="x", bufs=10)
            nc.vector.scalar_tensor_tensor(
                out=x[i][:],
                in0=mm_bank[i][:],
                scalar=1.0,
                in1=base[i][:],
                op0=ALU.mult,
                op1=ALU.add,
                accum_out=sums[m][:, j : j + 1],
            )
            nc.sync.dma_start(out=x_rows[m, j], in_=x[i][:])

        def square_sums(i):
            m, j = divmod(i, 2)
            if j == 0:
                squares[m] = work.tile([P, 2], F32, name="squares")
            deviations = work.tile([P, D], BF16, name="deviations")
            nc.scalar.activation(
                out=deviations[:],
                in_=x[i][:],
                func=ACT.Square,
                scale=-float(D),
                bias=sums[m][:, j : j + 1],
                accum_out=squares[m][:, j : j + 1],
            )

        def variance_of(m):
            variance[m] = work.tile([P, 2], F32, name="variance")
            nc.scalar.activation(
                out=variance[m][:], in_=squares[m][:], func=ACT.Identity, scale=1.0 / D**3, bias=EPS
            )

        def inverse_root(m):
            rstd[m] = work.tile([P, 2], F32, name="rstd")
            nc.gpsimd.tensor_tensor(out=rstd[m][:], in0=variance[m][:], in1=minus_half[:], op=ALU.pow)

        def shift_of(m):
            shift[m] = work.tile([P, 2], F32, name="shift")
            nc.vector.scalar_tensor_tensor(
                out=shift[m][:], in0=sums[m][:], scalar=-1.0 / D, in1=rstd[m][:], op0=ALU.mult, op1=ALU.mult
            )

        def normalise(i, engine, rows):
            m, j = divmod(i, 2)
            n_rows[i] = rows
            dst = rows[:].rearrange("r t (c e) -> r c t e", e=2)
            src = x[i][:].rearrange("r (c e t) -> r c t e", e=2, t=PACK)
            scale, bias = rstd[m][:, j : j + 1], shift[m][:, j : j + 1]
            if engine is nc.scalar:
                engine.activation(out=dst, in_=src, func=ACT.Identity, scale=scale, bias=bias)
            else:
                engine.tensor_scalar(out=dst, in0=src, scalar1=scale, scalar2=bias, op0=ALU.mult, op1=ALU.add)

        def normalise_on_gpsimd(m):
            normalise(2 * m, nc.gpsimd, stage_tile([P, PACK, P], F32, "n_rows_staged", 2 * m + 4))
            normalise(2 * m + 1, nc.gpsimd, work.tile([P, PACK, P], F32, name="n_rows1"))

        def normalise_shared(m):
            normalise(2 * m, nc.scalar, work.tile([P, PACK, P], F32, name="n_rows0"))
            normalise(2 * m + 1, nc.vector, work.tile([P, PACK, P], F32, name="n_rows1"))

        def transpose_n(m):
            n_banks[m] = [psum.tile([P, 2, 2 * P], F32, name="n_bank%d" % q) for q in range(2)]
            for t in range(PACK):
                for j in range(2):
                    nc.tensor.transpose(
                        n_banks[m][t // 2][:, t % 2, j * P : (j + 1) * P], n_rows[2 * m + j][:, t, :], ident[:]
                    )

        def gain_and_bias(m):
            h_planes[m] = work.tile([P, PACK, 2 * P], BF16, name="h_planes")
            for t in range(PACK):
                nc.scalar.activation(
                    out=h_planes[m][:, t, :],
                    in_=n_banks[m][t // 2][:, t % 2, :],
                    func=ACT.Identity,
                    scale=gain_col[:, t : t + 1],
                    bias=bias_col[:, t : t + 1],
                )

        def group_h_on_gpsimd(m):
            h_grouped[m] = stage_tile([P, 2 * P, PACK], BF16, "h_grouped_staged", 2 * m + 7)
            nc.gpsimd.tensor_scalar(
                out=h_grouped[m][:],
                in0=h_planes[m][:].rearrange("p t c -> p c t"),
                scalar1=1.0,
                scalar2=0.0,
                op0=ALU.mult,
                op1=ALU.add,
            )

        def group_h_on_vector(m):
            h_grouped[m] = work.tile([P, 2 * P, PACK], BF16, name="h_grouped", align_bytes=64)
            nc.vector.tensor_copy(
                out=h_grouped[m][:].rearrange("p (c i) t -> p c t i", i=4),
                in_=h_planes[m][:].rearrange("p t (c i) -> p c t i", i=4),
            )

        def quantize_h(m):
            h_codes[m] = work.tile([P, 2 * P], U32, name="h_codes", align_bytes=64)
            h_scales[m] = work.tile([P, 2 * P], U8, name="h_scales", align_bytes=64)
            nc.vector.quantize_mx(
                out=h_codes[m][:].bitcast(FP8X4),
                scales=h_scales[m][:],
                in_=h_grouped[m][:].rearrange("p c t -> p (c t)"),
            )

        def up_project(m):
            up_bank[m] = psum.tile([P, 2, F], F32, name="up_bank", tag="up_bank")
            for j in range(2):
                cols = slice(j * P, (j + 1) * P)
                nc.tensor.matmul_mx(
                    out=up_bank[m][:, j, :],
                    lhsT=h_codes[m][:, cols].bitcast(FP8X4),
                    lhsT_scale=h_scales[m][:, cols],
                    rhs=w1_codes[:].bitcast(FP8X4),
                    rhs_scale=w1_scales[:],
                    start=True,
                    stop=True,
                )

        def add_b1(m):
            pre_gelu[m] = work.tile([P, 2, F], F32, name="pre_gelu")
            nc.vector.tensor_tensor(
                out=pre_gelu[m][:],
                in0=up_bank[m][:],
                in1=b1_rows[:].unsqueeze(1).to_broadcast([P, 2, F]),
                op=ALU.add,
            )

        def gelu(m):
            g_rows = work.tile([P, 2 * F], F32, name="g_rows", bufs=3)
            nc.scalar.activation(
                out=g_rows[:], in_=pre_gelu[m][:].rearrange("r j f -> r (j f)"), func=ACT.Gelu_apprx_tanh
            )
            nc.sync.dma_start(out=g_pairs[m], in_=g_rows[:])

        def for_tile(stage, i):
            if 0 <= i < TILES:
                stage(i)

        def for_pair(stage, step, lag):
            m, odd = divmod(step - lag - 1, 2)
            if odd == 0 and 0 <= m < PAIRS:
                stage(m)

        for s in range(TILES + 11):
            for_tile(finish_x, s - 3)
            if s == 1:
                spread(bo_col, PACK, bo_rows)
            if s == 3:
                spread(b1_col, HALVES, b1_rows)
            if s == 2:
                turn_bo()
            if s - 2 < GPSIMD_BASE_TILES:
                for_tile(base_on_gpsimd, s - 2)
            else:
                for_tile(fetch_base, s - 2)
            if s <= TILES:
                for_pair(normalise_on_gpsimd, s, 5)
                for_pair(group_h_on_gpsimd, s, 8)
            for_pair(variance_of, s, 4)
            for_tile(group_attn, s - 1)
            for_pair(inverse_root, s, 4)
            for_tile(project, s - 2)
            for_pair(up_project, s, 9)
            if s - 1 >= GPSIMD_BASE_TILES:
                for_tile(base_on_tensor, s - 1)
            if s == 0:
                interleave_wo(0, 0)
                interleave_wo(1, 0)
                interleave_wo(0, 1)
            for_tile(scale_attn, s)
            if s == 0:
                interleave_wo(1, 1)
                quantize_wo(0, 0)
                quantize_wo(0, 1)
            if s == 1:
                quantize_wo(1, 1)
                quantize_wo(1, 0)
            if s == 2:
                interleave_w1()
            if s == 4:
                quantize_w1()
            for_pair(add_b1, s, 10)
            for_pair(gain_and_bias, s, 6)
            if s > TILES:
                for_pair(normalise_shared, s, 5)
            for_tile(square_sums, s - 3)
            for_tile(transpose_attn, s)
            for_pair(gelu, s, 11)
            for_pair(quantize_h, s, 8)
            for_pair(shift_of, s, 4)
            if s >= TILES:
                for_pair(group_h_on_vector, s, 7)
            for_tile(quantize_attn, s - 1)
            for_pair(transpose_n, s, 5)
